import numpy as np
import ml_dtypes


def mxq(x, axis, fmt="e4m3"):
    dtype, down = {"e4m3": (ml_dtypes.float8_e4m3fn, 7), "e5m2": (ml_dtypes.float8_e5m2, 14)}[fmt]
    v = np.moveaxis(np.asarray(x, np.float32).astype(ml_dtypes.bfloat16).astype(np.float64), axis, -1)
    blocks = v.reshape(v.shape[:-1] + (-1, 32))
    amax = np.abs(blocks).max(-1, keepdims=True)
    byte = np.maximum(np.where(amax > 0, np.frexp(amax)[1] - 1 + 127, 0) - down, 1)
    scale = np.exp2(byte - 127.0)
    codes = (blocks / scale).astype(np.float32).astype(dtype).astype(np.float64)
    return np.moveaxis((codes * scale).reshape(v.shape), -1, axis)


WIDE = False


def mx_kscale(k):
    if not WIDE:
        return np.ones(k)
    levels = np.array([10, -10, 5, -5, 0])
    if k % 512:
        return np.exp2(np.random.permutation(np.resize(levels, k // 32))).repeat(32)
    a = np.empty((k // 512, 16))
    for p in range(k // 512):
        a[p, :8] = np.random.permutation(np.resize(levels, 8))
        for g in range(8):
            far = levels[np.abs(levels - a[p, g]) >= 10]
            a[p, g + 8] = far[np.random.randint(len(far))]
    return np.exp2(a.ravel()).repeat(32)


BF16 = ml_dtypes.bfloat16


def bf(x):
    return np.asarray(x, np.float32).astype(BF16)


def f64(x):
    return np.asarray(x).astype(np.float64)


B, S, D, DFF, R = 4, 128, 1024, 4096, 512


def erf(z):
    z2 = z * z
    acc = np.zeros_like(z)
    for c in (np.arange(13) + 0.5) ** 2 * 0.25:
        acc += np.exp(-c) / (c + z2)
    return np.tanh(2.0 * np.pi * z) - z * np.exp(-z2) / np.pi * acc


def gelu_erf(v):
    return 0.5 * v * (1.0 + erf(v / np.sqrt(2.0)))


def setup_inputs():
    s, r = mx_kscale(D), mx_kscale(R)
    return {"x": bf(np.random.standard_normal((B, S, D)) * s),
            "c_fc_U": bf(np.random.standard_normal((D, R)) * 2.0 / np.sqrt(D) / s[:, None]),
            "c_fc_S": bf(np.random.uniform(size=R) * r),
            "c_fc_V": bf(np.random.standard_normal((DFF, R)) / np.sqrt(R) / r[None, :]),
            "c_fc_bias": bf(np.random.standard_normal(DFF) * 0.3)}


def reference(x, c_fc_U, c_fc_S, c_fc_V, c_fc_bias):
    us = f64(c_fc_U) * f64(c_fc_S)[None, :]
    w = mxq(us, 1, "e4m3") @ mxq(f64(c_fc_V), 1, "e4m3").T
    h = (mxq(f64(x), 2, "e4m3") @ mxq(w, 0, "e4m3")) + f64(c_fc_bias)
    return gelu_erf(h)

@@ -1,0 +1,214 @@
+from contextlib import ExitStack
+
+import concourse.mybir as mybir
+from concourse.masks import make_identity
+
+F32 = mybir.dt.float32
+BF16 = mybir.dt.bfloat16
+U32 = mybir.dt.uint32
+U8 = mybir.dt.uint8
+FP8X4 = mybir.dt.float8_e4m3fn_x4
+ACT = mybir.ActivationFunctionType
+ALU = mybir.AluOpType
+
+TOKENS, D, DFF, R = 512, 1024, 4096, 512
+P = 128
+CHUNK = 512
+N_CHUNKS = DFF // CHUNK
+FLOPS = 2 * D * DFF * R + 2 * TOKENS * DFF * D
+
+W_BANK_DTYPE = F32
+VECTOR_W_TILES = (0, 2, 5)
+
+
+def tile_hybridsuperlayer_pa_kernel(tc, x, c_fc_U, c_fc_S, c_fc_V, c_fc_bias, out):
+    nc = tc.nc
+    x_rows = x.flatten_outer_dims()
+    out_rows = out.flatten_outer_dims()
+    u_view = c_fc_U.rearrange("(g m t) r -> g m t r", g=2, t=4)
+    v_view = c_fc_V.rearrange("(c p j) r -> c p j r", c=N_CHUNKS, j=4)
+
+    with ExitStack() as ctx:
+        keep = ctx.enter_context(tc.tile_pool(name="keep", bufs=1))
+        vg_pool = ctx.enter_context(tc.tile_pool(name="vg", bufs=2))
+        vq_pool = ctx.enter_context(tc.tile_pool(name="vq", bufs=3))
+        wq_pool = ctx.enter_context(tc.tile_pool(name="wq", bufs=4))
+        ep_pool = ctx.enter_context(tc.tile_pool(name="ep", bufs=4))
+        tp_psum = ctx.enter_context(tc.psum_pool(name="tp", bufs=2))
+        w_psum = ctx.enter_context(tc.psum_pool(name="wp", bufs=4))
+        acc_psum = ctx.enter_context(tc.psum_pool(name="ac", bufs=2))
+        ctx.enter_context(tc.manual_schedule(engines={mybir.EngineType.PE}))
+
+        ident = keep.tile([P, P], F32)
+        make_identity(nc, ident[:])
+        warm_in = keep.tile([P, 1], F32)
+        warm_out = keep.tile([P, 1], F32)
+        nc.vector.memset(warm_in[:], 0.0)
+        nc.scalar.activation(out=warm_out[:], in_=warm_in[:], func=ACT.Gelu)
+
+        s_bc = keep.tile([P, R], BF16)
+        u_raw = [keep.tile([P, 4, R], BF16, name="u_raw%d" % g) for g in range(2)]
+        v_raw = [keep.tile([P, 4, R], BF16, name="v_raw%d" % c) for c in range(N_CHUNKS)]
+        x_raw = [keep.tile([P, D], BF16, name="x_raw%d" % i) for i in range(4)]
+        bias_bc = [keep.tile([P, DFF // 2], BF16, name="bias_bc%d" % b) for b in range(2)]
+
+        def load_v(c):
+            nc.sync.dma_start(out=v_raw[c][:], in_=v_view[c])
+
+        def load_bias(b):
+            half = DFF // 2
+            nc.sync.dma_start(out=bias_bc[b][:], in_=c_fc_bias[b * half : (b + 1) * half].partition_broadcast(P))
+
+        nc.sync.dma_start(out=s_bc[:], in_=c_fc_S.partition_broadcast(P))
+        for h in range(2):
+            nc.sync.dma_start(out=u_raw[0][:, 2 * h : 2 * h + 2, :], in_=u_view[0][:, 2 * h : 2 * h + 2, :])
+        for h in range(2):
+            nc.sync.dma_start(out=v_raw[0][:, 2 * h : 2 * h + 2, :], in_=v_view[0][:, 2 * h : 2 * h + 2, :])
+        nc.sync.dma_start(out=u_raw[1][:], in_=u_view[1])
+        load_v(1)
+        for i in range(4):
+            nc.sync.dma_start(out=x_raw[i][:], in_=x_rows[i * P : (i + 1) * P, :])
+        load_v(2)
+        load_bias(0)
+        load_v(3)
+        load_v(4)
+        load_bias(1)
+        load_v(5)
+        load_v(6)
+        load_v(7)
+
+        def copy_out(on_vector, dst, src):
+            if on_vector:
+                nc.vector.tensor_copy(out=dst, in_=src)
+            else:
+                nc.scalar.copy(out=dst, in_=src)
+
+        def transpose_bank(words):
+            bank = tp_psum.tile([P, 2, 2, P], F32, tag="tp_bank")
+            for s in range(2):
+                for u in range(2):
+                    nc.tensor.transpose(bank[:, s, u, :], words[s][u], ident[:])
+            return bank
+
+        def every_2nd_word(row_tile, first_word):
+            words = row_tile.bitcast(F32)
+            return [words[:, first_word + u : first_word + 256 : 2] for u in range(2)]
+
+        def quantize(grouped, name, pool):
+            codes = pool.tile([P, CHUNK], U32, tag=name + "_codes", name=name + "_codes", align_bytes=64)
+            scales = pool.tile([P, CHUNK], U8, tag=name + "_scales", name=name + "_scales", align_bytes=64)
+            nc.vector.quantize_mx(out=codes[:].bitcast(FP8X4), scales=scales[:], in_=grouped[:])
+            return codes, scales
+
+        us = [keep.tile([P, 4, R], BF16, name="us%d" % g) for g in range(2)]
+        us_grouped = [keep.tile([P, 4 * CHUNK], BF16, name="us_grouped%d" % g, align_bytes=64) for g in range(2)]
+        x_grouped = [keep.tile([P, 4 * CHUNK], BF16, name="x_grouped%d" % g, align_bytes=64) for g in range(2)]
+        us_q = {}
+        x_q = {}
+        v_grouped = {}
+        v_q = {}
+        w_grouped = {}
+        w_q = {}
+
+        def scale_u(g):
+            for t in range(4):
+                nc.vector.tensor_tensor(out=us[g][:, t, :], in0=u_raw[g][:, t, :], in1=s_bc[:], op=ALU.mult)
+
+        def grouped_half(grouped, h):
+            return grouped[:, 1024 * h : 1024 * (h + 1)].bitcast(F32).rearrange("p (s m u) -> p s m u", s=2, u=2)
+
+        def transpose_u(g):
+            for h in range(2):
+                bank = transpose_bank([every_2nd_word(us[g][:, 2 * h + s, :], 0) for s in range(2)])
+                copy_out(h == 1, grouped_half(us_grouped[g], h), bank[:].rearrange("p s u m -> p s m u"))
+
+        def transpose_x(g):
+            for h in range(2):
+                bank = transpose_bank([every_2nd_word(x_raw[2 * h + s][:], 256 * g) for s in range(2)])
+                copy_out(h == 1, grouped_half(x_grouped[g], h), bank[:].rearrange("p s u m -> p s m u"))
+
+        def transpose_v(c):
+            v_grouped[c] = vg_pool.tile([P, 4 * CHUNK], BF16, tag="v_grouped", name="v_grouped", align_bytes=64)
+            dst = v_grouped[c][:].bitcast(F32).rearrange("k (p j u) -> k p j u", j=4, u=2)
+            for h in range(2):
+                bank = transpose_bank([every_2nd_word(v_raw[c][:, 2 * h + s, :], 0) for s in range(2)])
+                copy_out(False, dst[:, :, 2 * h : 2 * h + 2, :], bank[:].rearrange("k j u p -> k p j u"))
+
+        def stage1_tile(c, n):
+            g, fs = n // 4, n % 4
+            if fs == 0:
+                w_grouped[(c, g)] = wq_pool.tile([P, 4 * CHUNK], BF16, tag="w_grouped", name="w_grouped", align_bytes=64)
+            u_codes, u_scales = us_q[g]
+            v_codes, v_scales = v_q[c]
+            w_bank = w_psum.tile([P, 4, P], W_BANK_DTYPE, tag="w_bank")
+            cols = slice(fs * P, (fs + 1) * P)
+            for t in range(4):
+                d_cols = slice(t * P, (t + 1) * P)
+                nc.tensor.matmul_mx(
+                    out=w_bank[:, t, :],
+                    lhsT=u_codes[:, d_cols].bitcast(FP8X4),
+                    lhsT_scale=u_scales[:, d_cols],
+                    rhs=v_codes[:, cols].bitcast(FP8X4),
+                    rhs_scale=v_scales[:, cols],
+                    start=True,
+                    stop=True,
+                )
+            dst = w_grouped[(c, g)][:, 4 * P * fs : 4 * P * (fs + 1)].rearrange("p (f t) -> p f t", t=4)
+            copy_out(n in VECTOR_W_TILES, dst, w_bank[:].rearrange("p t f -> p f t"))
+
+        def stage2_tile(c, i):
+            acc = acc_psum.tile([P, CHUNK], F32, tag="acc")
+            toks = slice(i * P, (i + 1) * P)
+            for g in range(2):
+                nc.tensor.matmul_mx(
+                    out=acc[:],
+                    lhsT=x_q[g][0][:, toks].bitcast(FP8X4),
+                    lhsT_scale=x_q[g][1][:, toks],
+                    rhs=w_q[(c, g)][0][:].bitcast(FP8X4),
+                    rhs_scale=w_q[(c, g)][1][:],
+                    start=(g == 0),
+                    stop=(g == 1),
+                )
+            h_sb = ep_pool.tile([P, CHUNK], F32, tag="h_sb")
+            b = c // (N_CHUNKS // 2)
+            b_cols = slice((c % (N_CHUNKS // 2)) * CHUNK, (c % (N_CHUNKS // 2) + 1) * CHUNK)
+            nc.vector.tensor_tensor(out=h_sb[:], in0=acc[:], in1=bias_bc[b][:, b_cols], op=ALU.add)
+            o_sb = ep_pool.tile([P, CHUNK], F32, tag="o_sb")
+            nc.scalar.activation(out=o_sb[:], in_=h_sb[:], func=ACT.Gelu)
+            nc.sync.dma_start(out=out_rows[toks, c * CHUNK : (c + 1) * CHUNK], in_=o_sb[:])
+
+        scale_u(0)
+        transpose_u(0)
+        transpose_v(0)
+        scale_u(1)
+        us_q[0] = quantize(us_grouped[0], "us0", keep)
+        transpose_u(1)
+        v_q[0] = quantize(v_grouped[0], "v", vq_pool)
+        us_q[1] = quantize(us_grouped[1], "us1", keep)
+        for n in range(4):
+            stage1_tile(0, n)
+        transpose_v(1)
+        w_q[(0, 0)] = quantize(w_grouped[(0, 0)], "w", wq_pool)
+        for n in range(4, 8):
+            stage1_tile(0, n)
+        v_q[1] = quantize(v_grouped[1], "v", vq_pool)
+        transpose_x(0)
+        w_q[(0, 1)] = quantize(w_grouped[(0, 1)], "w", wq_pool)
+        transpose_x(1)
+        x_q[0] = quantize(x_grouped[0], "x0", keep)
+        x_q[1] = quantize(x_grouped[1], "x1", keep)
+
+        for c in range(N_CHUNKS):
+            if c + 2 < N_CHUNKS:
+                transpose_v(c + 2)
+            for q in range(4):
+                if c + 1 < N_CHUNKS:
+                    stage1_tile(c + 1, 2 * q)
+                    stage1_tile(c + 1, 2 * q + 1)
+                stage2_tile(c, q)
+                if q == 0 and c + 2 < N_CHUNKS:
+                    v_q[c + 2] = quantize(v_grouped[c + 2], "v", vq_pool)
+                if q == 2 and c + 1 < N_CHUNKS:
+                    w_q[(c + 1, 0)] = quantize(w_grouped[(c + 1, 0)], "w", wq_pool)
+            if c + 1 < N_CHUNKS:
+                w_q[(c + 1, 1)] = quantize(w_grouped[(c + 1, 1)], "w", wq_pool)

@@ -19,6 +19,9 @@ FLOPS = 2 * D * DFF * R + 2 * TOKENS * DFF * D
 
 W_BANK_DTYPE = F32
 VECTOR_W_TILES = (0, 2, 5)
+N_SLOTS = 4 * N_CHUNKS
+LAG = 6
+X_SLOT = 2
 
 
 def tile_hybridsuperlayer_pa_kernel(tc, x, c_fc_U, c_fc_S, c_fc_V, c_fc_bias, out):
@@ -32,12 +35,10 @@ def tile_hybridsuperlayer_pa_kernel(tc, x, c_fc_U, c_fc_S, c_fc_V, c_fc_bias, ou
         keep = ctx.enter_context(tc.tile_pool(name="keep", bufs=1))
         vg_pool = ctx.enter_context(tc.tile_pool(name="vg", bufs=2))
         vq_pool = ctx.enter_context(tc.tile_pool(name="vq", bufs=3))
-        wq_pool = ctx.enter_context(tc.tile_pool(name="wq", bufs=4))
-        ep_pool = ctx.enter_context(tc.tile_pool(name="ep", bufs=4))
-        tp_psum = ctx.enter_context(tc.psum_pool(name="tp", bufs=2))
-        w_psum = ctx.enter_context(tc.psum_pool(name="wp", bufs=4))
-        acc_psum = ctx.enter_context(tc.psum_pool(name="ac", bufs=2))
-        ctx.enter_context(tc.manual_schedule(engines={mybir.EngineType.PE}))
+        wq_pool = ctx.enter_context(tc.tile_pool(name="wq", bufs=6))
+        ep_pool = ctx.enter_context(tc.tile_pool(name="ep", bufs=6))
+        psum = ctx.enter_context(tc.psum_pool(name="psum", bufs=8))
+        ctx.enter_context(tc.manual_schedule())
 
         ident = keep.tile([P, P], F32)
         make_identity(nc, ident[:])
@@ -84,7 +85,7 @@ def tile_hybridsuperlayer_pa_kernel(tc, x, c_fc_U, c_fc_S, c_fc_V, c_fc_bias, ou
                 nc.scalar.copy(out=dst, in_=src)
 
         def transpose_bank(words):
-            bank = tp_psum.tile([P, 2, 2, P], F32, tag="tp_bank")
+            bank = psum.tile([P, 2, 2, P], F32, tag="bank", name="tp_bank")
             for s in range(2):
                 for u in range(2):
                     nc.tensor.transpose(bank[:, s, u, :], words[s][u], ident[:])
@@ -109,6 +110,7 @@ def tile_hybridsuperlayer_pa_kernel(tc, x, c_fc_U, c_fc_S, c_fc_V, c_fc_bias, ou
         v_q = {}
         w_grouped = {}
         w_q = {}
+        h_tiles = {}
 
         def scale_u(g):
             for t in range(4):
@@ -120,12 +122,12 @@ def tile_hybridsuperlayer_pa_kernel(tc, x, c_fc_U, c_fc_S, c_fc_V, c_fc_bias, ou
         def transpose_u(g):
             for h in range(2):
                 bank = transpose_bank([every_2nd_word(us[g][:, 2 * h + s, :], 0) for s in range(2)])
-                copy_out(h == 1, grouped_half(us_grouped[g], h), bank[:].rearrange("p s u m -> p s m u"))
+                copy_out(h == 0, grouped_half(us_grouped[g], h), bank[:].rearrange("p s u m -> p s m u"))
 
         def transpose_x(g):
             for h in range(2):
                 bank = transpose_bank([every_2nd_word(x_raw[2 * h + s][:], 256 * g) for s in range(2)])
-                copy_out(h == 1, grouped_half(x_grouped[g], h), bank[:].rearrange("p s u m -> p s m u"))
+                copy_out(h == 0, grouped_half(x_grouped[g], h), bank[:].rearrange("p s u m -> p s m u"))
 
         def transpose_v(c):
             v_grouped[c] = vg_pool.tile([P, 4 * CHUNK], BF16, tag="v_grouped", name="v_grouped", align_bytes=64)
@@ -140,7 +142,7 @@ def tile_hybridsuperlayer_pa_kernel(tc, x, c_fc_U, c_fc_S, c_fc_V, c_fc_bias, ou
                 w_grouped[(c, g)] = wq_pool.tile([P, 4 * CHUNK], BF16, tag="w_grouped", name="w_grouped", align_bytes=64)
             u_codes, u_scales = us_q[g]
             v_codes, v_scales = v_q[c]
-            w_bank = w_psum.tile([P, 4, P], W_BANK_DTYPE, tag="w_bank")
+            w_bank = psum.tile([P, 4, P], W_BANK_DTYPE, tag="bank", name="w_bank")
             cols = slice(fs * P, (fs + 1) * P)
             for t in range(4):
                 d_cols = slice(t * P, (t + 1) * P)
@@ -156,8 +158,9 @@ def tile_hybridsuperlayer_pa_kernel(tc, x, c_fc_U, c_fc_S, c_fc_V, c_fc_bias, ou
             dst = w_grouped[(c, g)][:, 4 * P * fs : 4 * P * (fs + 1)].rearrange("p (f t) -> p f t", t=4)
             copy_out(n in VECTOR_W_TILES, dst, w_bank[:].rearrange("p t f -> p f t"))
 
-        def stage2_tile(c, i):
-            acc = acc_psum.tile([P, CHUNK], F32, tag="acc")
+        def stage2_tile(k):
+            c, i = k // 4, k % 4
+            acc = psum.tile([P, CHUNK], F32, tag="bank", name="acc")
             toks = slice(i * P, (i + 1) * P)
             for g in range(2):
                 nc.tensor.matmul_mx(
@@ -169,46 +172,47 @@ def tile_hybridsuperlayer_pa_kernel(tc, x, c_fc_U, c_fc_S, c_fc_V, c_fc_bias, ou
                     start=(g == 0),
                     stop=(g == 1),
                 )
-            h_sb = ep_pool.tile([P, CHUNK], F32, tag="h_sb")
+            h_tiles[k] = ep_pool.tile([P, CHUNK], F32, tag="h_sb", name="h_sb")
             b = c // (N_CHUNKS // 2)
             b_cols = slice((c % (N_CHUNKS // 2)) * CHUNK, (c % (N_CHUNKS // 2) + 1) * CHUNK)
-            nc.vector.tensor_tensor(out=h_sb[:], in0=acc[:], in1=bias_bc[b][:, b_cols], op=ALU.add)
+            nc.vector.tensor_tensor(out=h_tiles[k][:], in0=acc[:], in1=bias_bc[b][:, b_cols], op=ALU.add)
+
+        def gelu_and_store(k):
+            c, i = k // 4, k % 4
             o_sb = ep_pool.tile([P, CHUNK], F32, tag="o_sb")
-            nc.scalar.activation(out=o_sb[:], in_=h_sb[:], func=ACT.Gelu)
-            nc.sync.dma_start(out=out_rows[toks, c * CHUNK : (c + 1) * CHUNK], in_=o_sb[:])
+            nc.scalar.activation(out=o_sb[:], in_=h_tiles[k][:], func=ACT.Gelu)
+            nc.sync.dma_start(out=out_rows[i * P : (i + 1) * P, c * CHUNK : (c + 1) * CHUNK], in_=o_sb[:])
 
         scale_u(0)
         transpose_u(0)
+        us_q[0] = quantize(us_grouped[0], "us0", keep)
         transpose_v(0)
         scale_u(1)
-        us_q[0] = quantize(us_grouped[0], "us0", keep)
-        transpose_u(1)
         v_q[0] = quantize(v_grouped[0], "v", vq_pool)
+        transpose_u(1)
         us_q[1] = quantize(us_grouped[1], "us1", keep)
-        for n in range(4):
-            stage1_tile(0, n)
-        transpose_v(1)
-        w_q[(0, 0)] = quantize(w_grouped[(0, 0)], "w", wq_pool)
-        for n in range(4, 8):
-            stage1_tile(0, n)
-        v_q[1] = quantize(v_grouped[1], "v", vq_pool)
-        transpose_x(0)
-        w_q[(0, 1)] = quantize(w_grouped[(0, 1)], "w", wq_pool)
-        transpose_x(1)
-        x_q[0] = quantize(x_grouped[0], "x0", keep)
-        x_q[1] = quantize(x_grouped[1], "x1", keep)
 
-        for c in range(N_CHUNKS):
-            if c + 2 < N_CHUNKS:
-                transpose_v(c + 2)
-            for q in range(4):
-                if c + 1 < N_CHUNKS:
-                    stage1_tile(c + 1, 2 * q)
-                    stage1_tile(c + 1, 2 * q + 1)
-                stage2_tile(c, q)
-                if q == 0 and c + 2 < N_CHUNKS:
-                    v_q[c + 2] = quantize(v_grouped[c + 2], "v", vq_pool)
-                if q == 2 and c + 1 < N_CHUNKS:
-                    w_q[(c + 1, 0)] = quantize(w_grouped[(c + 1, 0)], "w", wq_pool)
-            if c + 1 < N_CHUNKS:
-                w_q[(c + 1, 1)] = quantize(w_grouped[(c + 1, 1)], "w", wq_pool)
+        for s in range(N_SLOTS + LAG):
+            if s < N_SLOTS:
+                c, q = s // 4, s % 4
+                if q == 0 and c + 1 < N_CHUNKS:
+                    transpose_v(c + 1)
+                stage1_tile(c, 2 * q)
+                stage1_tile(c, 2 * q + 1)
+                if q == 1 and c + 1 < N_CHUNKS:
+                    v_q[c + 1] = quantize(v_grouped[c + 1], "v", vq_pool)
+                if q == 2:
+                    w_q[(c, 0)] = quantize(w_grouped[(c, 0)], "w", wq_pool)
+            if 0 < s <= N_SLOTS and s % 4 == 0:
+                w_q[(s // 4 - 1, 1)] = quantize(w_grouped[(s // 4 - 1, 1)], "w", wq_pool)
+            if s == X_SLOT:
+                for g in range(2):
+                    transpose_x(g)
+                for g in range(2):
+                    x_q[g] = quantize(x_grouped[g], "x%d" % g, keep)
+            k = s - LAG
+            if k >= 0:
+                stage2_tile(k)
+                if k >= 1:
+                    gelu_and_store(k - 1)
+        gelu_and_store(N_SLOTS - 1)

@@ -21,7 +21,9 @@ W_BANK_DTYPE = F32
 VECTOR_W_TILES = (0, 2, 5)
 N_SLOTS = 4 * N_CHUNKS
 LAG = 6
-X_SLOT = 2
+X_SLOTS = (1, 2)
+WARM_FIRST = 8
+WARM_BETWEEN = 2
 
 
 def tile_hybridsuperlayer_pa_kernel(tc, x, c_fc_U, c_fc_S, c_fc_V, c_fc_bias, out):
@@ -40,6 +42,8 @@ def tile_hybridsuperlayer_pa_kernel(tc, x, c_fc_U, c_fc_S, c_fc_V, c_fc_bias, ou
         psum = ctx.enter_context(tc.psum_pool(name="psum", bufs=8))
         ctx.enter_context(tc.manual_schedule())
 
+        zeros = keep.tile([P, CHUNK], BF16)
+        nc.gpsimd.memset(zeros[:], 0.0)
         ident = keep.tile([P, P], F32)
         make_identity(nc, ident[:])
         warm_in = keep.tile([P, 1], F32)
@@ -183,13 +187,22 @@ def tile_hybridsuperlayer_pa_kernel(tc, x, c_fc_U, c_fc_S, c_fc_V, c_fc_bias, ou
             nc.scalar.activation(out=o_sb[:], in_=h_tiles[k][:], func=ACT.Gelu)
             nc.sync.dma_start(out=out_rows[i * P : (i + 1) * P, c * CHUNK : (c + 1) * CHUNK], in_=o_sb[:])
 
+        def keep_tensor_busy(n):
+            idle_bank = psum.tile([P, CHUNK], F32, tag="bank", name="idle_bank")
+            for i in range(n):
+                nc.tensor.matmul(out=idle_bank[:], lhsT=zeros[:, 0:P], rhs=zeros[:], start=True, stop=True)
+
+        keep_tensor_busy(WARM_FIRST)
         scale_u(0)
         transpose_u(0)
+        keep_tensor_busy(WARM_BETWEEN)
         us_q[0] = quantize(us_grouped[0], "us0", keep)
         transpose_v(0)
+        keep_tensor_busy(WARM_BETWEEN)
         scale_u(1)
         v_q[0] = quantize(v_grouped[0], "v", vq_pool)
         transpose_u(1)
+        keep_tensor_busy(WARM_BETWEEN)
         us_q[1] = quantize(us_grouped[1], "us1", keep)
 
         for s in range(N_SLOTS + LAG):
@@ -205,10 +218,9 @@ def tile_hybridsuperlayer_pa_kernel(tc, x, c_fc_U, c_fc_S, c_fc_V, c_fc_bias, ou
                     w_q[(c, 0)] = quantize(w_grouped[(c, 0)], "w", wq_pool)
             if 0 < s <= N_SLOTS and s % 4 == 0:
                 w_q[(s // 4 - 1, 1)] = quantize(w_grouped[(s // 4 - 1, 1)], "w", wq_pool)
-            if s == X_SLOT:
-                for g in range(2):
+            for g in range(2):
+                if s == X_SLOTS[g]:
                     transpose_x(g)
-                for g in range(2):
                     x_q[g] = quantize(x_grouped[g], "x%d" % g, keep)
             k = s - LAG
             if k >= 0:

from contextlib import ExitStack

import concourse.mybir as mybir
from concourse.masks import make_identity

F32 = mybir.dt.float32
BF16 = mybir.dt.bfloat16
U32 = mybir.dt.uint32
U8 = mybir.dt.uint8
FP8X4 = mybir.dt.float8_e4m3fn_x4
ACT = mybir.ActivationFunctionType
ALU = mybir.AluOpType

TOKENS, D, DFF, R = 512, 1024, 4096, 512
P = 128
CHUNK = 512
N_CHUNKS = DFF // CHUNK
FLOPS = 2 * D * DFF * R + 2 * TOKENS * DFF * D

W_BANK_DTYPE = F32
VECTOR_W_TILES = (0, 2, 5)
N_SLOTS = 4 * N_CHUNKS
LAG = 6
X_SLOTS = (1, 2)
WARM_FIRST = 8
WARM_BETWEEN = 2


def tile_hybridsuperlayer_pa_kernel(tc, x, c_fc_U, c_fc_S, c_fc_V, c_fc_bias, out):
    nc = tc.nc
    x_rows = x.flatten_outer_dims()
    out_rows = out.flatten_outer_dims()
    u_view = c_fc_U.rearrange("(g m t) r -> g m t r", g=2, t=4)
    v_view = c_fc_V.rearrange("(c p j) r -> c p j r", c=N_CHUNKS, j=4)

    with ExitStack() as ctx:
        keep = ctx.enter_context(tc.tile_pool(name="keep", bufs=1))
        vg_pool = ctx.enter_context(tc.tile_pool(name="vg", bufs=2))
        vq_pool = ctx.enter_context(tc.tile_pool(name="vq", bufs=3))
        wq_pool = ctx.enter_context(tc.tile_pool(name="wq", bufs=6))
        ep_pool = ctx.enter_context(tc.tile_pool(name="ep", bufs=6))
        psum = ctx.enter_context(tc.psum_pool(name="psum", bufs=8))
        ctx.enter_context(tc.manual_schedule())

        zeros = keep.tile([P, CHUNK], BF16)
        nc.gpsimd.memset(zeros[:], 0.0)
        ident = keep.tile([P, P], F32)
        make_identity(nc, ident[:])
        warm_in = keep.tile([P, 1], F32)
        warm_out = keep.tile([P, 1], F32)
        nc.vector.memset(warm_in[:], 0.0)
        nc.scalar.activation(out=warm_out[:], in_=warm_in[:], func=ACT.Gelu)

        s_bc = keep.tile([P, R], BF16)
        u_raw = [keep.tile([P, 4, R], BF16, name="u_raw%d" % g) for g in range(2)]
        v_raw = [keep.tile([P, 4, R], BF16, name="v_raw%d" % c) for c in range(N_CHUNKS)]
        x_raw = [keep.tile([P, D], BF16, name="x_raw%d" % i) for i in range(4)]
        bias_bc = [keep.tile([P, DFF // 2], BF16, name="bias_bc%d" % b) for b in range(2)]

        def load_v(c):
            nc.sync.dma_start(out=v_raw[c][:], in_=v_view[c])

        def load_bias(b):
            half = DFF // 2
            nc.sync.dma_start(out=bias_bc[b][:], in_=c_fc_bias[b * half : (b + 1) * half].partition_broadcast(P))

        nc.sync.dma_start(out=s_bc[:], in_=c_fc_S.partition_broadcast(P))
        for h in range(2):
            nc.sync.dma_start(out=u_raw[0][:, 2 * h : 2 * h + 2, :], in_=u_view[0][:, 2 * h : 2 * h + 2, :])
        for h in range(2):
            nc.sync.dma_start(out=v_raw[0][:, 2 * h : 2 * h + 2, :], in_=v_view[0][:, 2 * h : 2 * h + 2, :])
        nc.sync.dma_start(out=u_raw[1][:], in_=u_view[1])
        load_v(1)
        for i in range(4):
            nc.sync.dma_start(out=x_raw[i][:], in_=x_rows[i * P : (i + 1) * P, :])
        load_v(2)
        load_bias(0)
        load_v(3)
        load_v(4)
        load_bias(1)
        load_v(5)
        load_v(6)
        load_v(7)

        def copy_out(on_vector, dst, src):
            if on_vector:
                nc.vector.tensor_copy(out=dst, in_=src)
            else:
                nc.scalar.copy(out=dst, in_=src)

        def transpose_bank(words):
            bank = psum.tile([P, 2, 2, P], F32, tag="bank", name="tp_bank")
            for s in range(2):
                for u in range(2):
                    nc.tensor.transpose(bank[:, s, u, :], words[s][u], ident[:])
            return bank

        def every_2nd_word(row_tile, first_word):
            words = row_tile.bitcast(F32)
            return [words[:, first_word + u : first_word + 256 : 2] for u in range(2)]

        def quantize(grouped, name, pool):
            codes = pool.tile([P, CHUNK], U32, tag=name + "_codes", name=name + "_codes", align_bytes=64)
            scales = pool.tile([P, CHUNK], U8, tag=name + "_scales", name=name + "_scales", align_bytes=64)
            nc.vector.quantize_mx(out=codes[:].bitcast(FP8X4), scales=scales[:], in_=grouped[:])
            return codes, scales

        us = [keep.tile([P, 4, R], BF16, name="us%d" % g) for g in range(2)]
        us_grouped = [keep.tile([P, 4 * CHUNK], BF16, name="us_grouped%d" % g, align_bytes=64) for g in range(2)]
        x_grouped = [keep.tile([P, 4 * CHUNK], BF16, name="x_grouped%d" % g, align_bytes=64) for g in range(2)]
        us_q = {}
        x_q = {}
        v_grouped = {}
        v_q = {}
        w_grouped = {}
        w_q = {}
        h_tiles = {}

        def scale_u(g):
            for t in range(4):
                nc.vector.tensor_tensor(out=us[g][:, t, :], in0=u_raw[g][:, t, :], in1=s_bc[:], op=ALU.mult)

        def grouped_half(grouped, h):
            return grouped[:, 1024 * h : 1024 * (h + 1)].bitcast(F32).rearrange("p (s m u) -> p s m u", s=2, u=2)

        def transpose_u(g):
            for h in range(2):
                bank = transpose_bank([every_2nd_word(us[g][:, 2 * h + s, :], 0) for s in range(2)])
                copy_out(h == 0, grouped_half(us_grouped[g], h), bank[:].rearrange("p s u m -> p s m u"))

        def transpose_x(g):
            for h in range(2):
                bank = transpose_bank([every_2nd_word(x_raw[2 * h + s][:], 256 * g) for s in range(2)])
                copy_out(h == 0, grouped_half(x_grouped[g], h), bank[:].rearrange("p s u m -> p s m u"))

        def transpose_v(c):
            v_grouped[c] = vg_pool.tile([P, 4 * CHUNK], BF16, tag="v_grouped", name="v_grouped", align_bytes=64)
            dst = v_grouped[c][:].bitcast(F32).rearrange("k (p j u) -> k p j u", j=4, u=2)
            for h in range(2):
                bank = transpose_bank([every_2nd_word(v_raw[c][:, 2 * h + s, :], 0) for s in range(2)])
                copy_out(False, dst[:, :, 2 * h : 2 * h + 2, :], bank[:].rearrange("k j u p -> k p j u"))

        def stage1_tile(c, n):
            g, fs = n // 4, n % 4
            if fs == 0:
                w_grouped[(c, g)] = wq_pool.tile([P, 4 * CHUNK], BF16, tag="w_grouped", name="w_grouped", align_bytes=64)
            u_codes, u_scales = us_q[g]
            v_codes, v_scales = v_q[c]
            w_bank = psum.tile([P, 4, P], W_BANK_DTYPE, tag="bank", name="w_bank")
            cols = slice(fs * P, (fs + 1) * P)
            for t in range(4):
                d_cols = slice(t * P, (t + 1) * P)
                nc.tensor.matmul_mx(
                    out=w_bank[:, t, :],
                    lhsT=u_codes[:, d_cols].bitcast(FP8X4),
                    lhsT_scale=u_scales[:, d_cols],
                    rhs=v_codes[:, cols].bitcast(FP8X4),
                    rhs_scale=v_scales[:, cols],
                    start=True,
                    stop=True,
                )
            dst = w_grouped[(c, g)][:, 4 * P * fs : 4 * P * (fs + 1)].rearrange("p (f t) -> p f t", t=4)
            copy_out(n in VECTOR_W_TILES, dst, w_bank[:].rearrange("p t f -> p f t"))

        def stage2_tile(k):
            c, i = k // 4, k % 4
            acc = psum.tile([P, CHUNK], F32, tag="bank", name="acc")
            toks = slice(i * P, (i + 1) * P)
            for g in range(2):
                nc.tensor.matmul_mx(
                    out=acc[:],
                    lhsT=x_q[g][0][:, toks].bitcast(FP8X4),
                    lhsT_scale=x_q[g][1][:, toks],
                    rhs=w_q[(c, g)][0][:].bitcast(FP8X4),
                    rhs_scale=w_q[(c, g)][1][:],
                    start=(g == 0),
                    stop=(g == 1),
                )
            h_tiles[k] = ep_pool.tile([P, CHUNK], F32, tag="h_sb", name="h_sb")
            b = c // (N_CHUNKS // 2)
            b_cols = slice((c % (N_CHUNKS // 2)) * CHUNK, (c % (N_CHUNKS // 2) + 1) * CHUNK)
            nc.vector.tensor_tensor(out=h_tiles[k][:], in0=acc[:], in1=bias_bc[b][:, b_cols], op=ALU.add)

        def gelu_and_store(k):
            c, i = k // 4, k % 4
            o_sb = ep_pool.tile([P, CHUNK], F32, tag="o_sb")
            nc.scalar.activation(out=o_sb[:], in_=h_tiles[k][:], func=ACT.Gelu)
            nc.sync.dma_start(out=out_rows[i * P : (i + 1) * P, c * CHUNK : (c + 1) * CHUNK], in_=o_sb[:])

        def keep_tensor_busy(n):
            idle_bank = psum.tile([P, CHUNK], F32, tag="bank", name="idle_bank")
            for i in range(n):
                nc.tensor.matmul(out=idle_bank[:], lhsT=zeros[:, 0:P], rhs=zeros[:], start=True, stop=True)

        keep_tensor_busy(WARM_FIRST)
        scale_u(0)
        transpose_u(0)
        keep_tensor_busy(WARM_BETWEEN)
        us_q[0] = quantize(us_grouped[0], "us0", keep)
        transpose_v(0)
        keep_tensor_busy(WARM_BETWEEN)
        scale_u(1)
        v_q[0] = quantize(v_grouped[0], "v", vq_pool)
        transpose_u(1)
        keep_tensor_busy(WARM_BETWEEN)
        us_q[1] = quantize(us_grouped[1], "us1", keep)

        for s in range(N_SLOTS + LAG):
            if s < N_SLOTS:
                c, q = s // 4, s % 4
                if q == 0 and c + 1 < N_CHUNKS:
                    transpose_v(c + 1)
                stage1_tile(c, 2 * q)
                stage1_tile(c, 2 * q + 1)
                if q == 1 and c + 1 < N_CHUNKS:
                    v_q[c + 1] = quantize(v_grouped[c + 1], "v", vq_pool)
                if q == 2:
                    w_q[(c, 0)] = quantize(w_grouped[(c, 0)], "w", wq_pool)
            if 0 < s <= N_SLOTS and s % 4 == 0:
                w_q[(s // 4 - 1, 1)] = quantize(w_grouped[(s // 4 - 1, 1)], "w", wq_pool)
            for g in range(2):
                if s == X_SLOTS[g]:
                    transpose_x(g)
                    x_q[g] = quantize(x_grouped[g], "x%d" % g, keep)
            k = s - LAG
            if k >= 0:
                stage2_tile(k)
                if k >= 1:
                    gelu_and_store(k - 1)
        gelu_and_store(N_SLOTS - 1)
